import numpy as np
import ml_dtypes


def mxq(x, axis, fmt="e4m3"):
    dtype, down = {"e4m3": (ml_dtypes.float8_e4m3fn, 7), "e5m2": (ml_dtypes.float8_e5m2, 14)}[fmt]
    v = np.moveaxis(np.asarray(x, np.float32).astype(ml_dtypes.bfloat16).astype(np.float64), axis, -1)
    blocks = v.reshape(v.shape[:-1] + (-1, 32))
    amax = np.abs(blocks).max(-1, keepdims=True)
    byte = np.maximum(np.where(amax > 0, np.frexp(amax)[1] - 1 + 127, 0) - down, 1)
    scale = np.exp2(byte - 127.0)
    codes = (blocks / scale).astype(np.float32).astype(dtype).astype(np.float64)
    return np.moveaxis((codes * scale).reshape(v.shape), -1, axis)


WIDE = False


def mx_kscale(k):
    if not WIDE:
        return np.ones(k)
    levels = np.array([10, -10, 5, -5, 0])
    a = np.random.permutation(np.resize(levels, k // 512 * 4)).reshape(k // 512, 4)
    idx = np.arange(k)
    return np.exp2(a[idx // 512, idx % 128 // 32])


BF16 = ml_dtypes.bfloat16


def bf(x):
    return np.asarray(x, np.float32).astype(BF16)


def f64(x):
    return np.asarray(x).astype(np.float64)


E2M1 = np.array([0.0, 0.5, 1.0, 1.5, 2.0, 3.0, 4.0, 6.0, -0.0, -0.5, -1.0, -1.5, -2.0, -3.0, -4.0, -6.0])


def pack_weight(w, fmt):
    k, n = w.shape
    w = f64(bf(w)).reshape(k // 32, 32, n)
    amax = np.abs(w).max(1)
    if fmt == "e4m3":
        byte = np.frexp(amax)[1] - 1 + 127 - 7
    else:
        mant, ex = np.frexp(amax / 6.0)
        byte = np.where(mant > 0.5, ex, ex - 1) + 127
    byte = np.clip(np.where(amax > 0, byte, 1), 1, 254)
    scaled = (w * np.exp2(127.0 - byte)[:, None, :]).reshape(k, n).astype(np.float32)
    by_word = np.ascontiguousarray(scaled.reshape(k // 512, 128, 4, n).transpose(0, 1, 3, 2))
    if fmt == "e4m3":
        words = by_word.astype(ml_dtypes.float8_e4m3fn).view(np.uint8)
    else:
        c = by_word.astype(ml_dtypes.float4_e2m1fn).view(np.uint8) & 0xF
        words = c[..., 0::2] | (c[..., 1::2] << 4)
    return np.ascontiguousarray(words), np.ascontiguousarray(byte.astype(np.uint8).reshape(k // 512, 16, n))


def unpack_weight(words, scales, fmt):
    g, p, n, _ = words.shape
    if fmt == "e4m3":
        vals = np.ascontiguousarray(words).view(ml_dtypes.float8_e4m3fn).astype(np.float64)
    else:
        nib = np.empty((g, p, n, 4), np.uint8)
        nib[..., 0::2] = words & 0xF
        nib[..., 1::2] = words >> 4
        vals = E2M1[nib]
    vals = vals * np.repeat(np.exp2(scales.astype(np.float64) - 127.0), 8, axis=1)[..., None]
    return vals.transpose(0, 1, 3, 2).reshape(g * 512, n)


B, C_IN, H, W, C_OUT = 2, 512, 64, 64, 512
E = 1


def _box_sum(x):
    b, h, w, c = x.shape
    xp = np.pad(x, ((0, 0), (1, 1), (1, 1), (0, 0)))
    out = np.zeros_like(x)
    for i in range(3):
        for j in range(3):
            out = out + xp[:, i:i + h, j:j + w, :]
    return out


def setup_inputs():
    s = mx_kscale(C_IN)
    x = bf(np.random.standard_normal((B, C_IN, H, W)) * s[None, :, None, None])
    stack = np.random.standard_normal((E, C_IN, C_OUT)) * 3.0 / np.sqrt(C_IN) / s[None, :, None]
    words, scales = pack_weight(stack.reshape(-1, C_OUT), "e4m3")
    return {"x": x, "weight_words": words, "weight_scales": scales}


def reference(x, weight_words, weight_scales):
    x = f64(x)
    weight = unpack_weight(weight_words, weight_scales, "e4m3").reshape(E, C_IN, C_OUT)
    b, c, h, w = x.shape
    o = weight.shape[-1]
    x1 = np.transpose(x, (0, 2, 3, 1))
    xw = mxq(x1, 3, "e4m3") @ weight[0]
    deg = _box_sum(np.ones((1, h, w, 1)))
    dinv = 1.0 / np.sqrt(deg)
    y = dinv * _box_sum(dinv * xw)
    return np.transpose(y, (0, 3, 1, 2)).reshape(b, o, w, h)

@@ -1,0 +1,157 @@
+from contextlib import ExitStack
+import math
+
+import concourse.mybir as mybir
+
+BF16 = mybir.dt.bfloat16
+F32 = mybir.dt.float32
+I32 = mybir.dt.int32
+U32 = mybir.dt.uint32
+U8 = mybir.dt.uint8
+FP8X4 = mybir.dt.float8_e4m3fn_x4
+ADD = mybir.AluOpType.add
+
+P = 128
+PACK = 4
+B, C_IN, H, W, C_OUT = 2, 512, 64, 64, 512
+O_TILES = C_OUT // P
+ROWS = 16
+STEPS_PER_IMAGE = H // ROWS
+BANK_ROWS = 8
+HALF = W // 2
+AHEAD = 2
+
+BORDER = math.sqrt(1.5)
+NINTH = 1.0 / 9.0
+
+ROW_PITCH = 2 * (HALF + 2)
+ODD = slice(1, 1 + HALF)
+EVEN = slice(1 + HALF, 1 + W)
+
+FLOPS = 2 * B * H * W * C_IN * C_OUT
+
+
+def tile_gcn_layer_e_kernel(tc, x, weight_words, weight_scales, out):
+    nc = tc.nc
+    with ExitStack() as ctx:
+        keep = ctx.enter_context(tc.tile_pool(name="keep", bufs=1))
+        raw_pool = ctx.enter_context(tc.tile_pool(name="raw", bufs=4))
+        grouped_pool = ctx.enter_context(tc.tile_pool(name="grouped", bufs=2))
+        work = ctx.enter_context(tc.tile_pool(name="work", bufs=2))
+        result_pool = ctx.enter_context(tc.tile_pool(name="result", bufs=3))
+        psum = ctx.enter_context(tc.psum_pool(name="psum", bufs=8))
+
+        w_codes = keep.tile([P, C_OUT], U32, align_bytes=64)
+        w_scales = keep.tile([P, C_OUT], U8, align_bytes=64)
+        nc.vector.memset(w_scales[:].bitcast(I32), 0)
+        nc.sync.dma_start(
+            out=w_codes[:].bitcast(I32),
+            in_=weight_words[0].rearrange("p n t -> p (n t)").bitcast(I32),
+        )
+        for quadrant in range(4):
+            nc.sync.dma_start(
+                out=w_scales[32 * quadrant : 32 * quadrant + 4, :].bitcast(I32),
+                in_=weight_scales[0, 4 * quadrant : 4 * quadrant + 4, :].bitcast(I32),
+            )
+
+        x_codes = keep.tile([P, B, (H + 2) * W], U32, align_bytes=64)
+        x_scales = keep.tile([P, B, (H + 2) * W], U8, align_bytes=64)
+        for padded in (x_codes, x_scales):
+            zero_rows = padded[:].rearrange("p b (r w) -> p b r w", w=W)[:, :, 0 : H + 2 : H + 1, :]
+            nc.vector.memset(zero_rows.bitcast(I32), 0)
+
+        def quantise_rows(b, step):
+            pixels = slice(step * ROWS * W, (step + 1) * ROWS * W)
+            raw = raw_pool.tile([P, PACK, ROWS * W], BF16)
+            nc.sync.dma_start(out=raw[:], in_=x[b].rearrange("(p t) h w -> p t (h w)", t=PACK)[:, :, pixels])
+            grouped = grouped_pool.tile([P, ROWS * W, PACK], BF16, align_bytes=64)
+            nc.scalar.copy(
+                out=grouped[:].rearrange("p (c i) t -> p c t i", i=4),
+                in_=raw[:].rearrange("p t (c i) -> p c t i", i=4),
+            )
+            columns = slice((step * ROWS + 1) * W, ((step + 1) * ROWS + 1) * W)
+            nc.vector.quantize_mx(
+                out=x_codes[:, b, columns].bitcast(FP8X4),
+                scales=x_scales[:, b, columns],
+                in_=grouped[:].rearrange("p n t -> p (n t)"),
+            )
+
+        def multiply(acc, b, o, first_padded_row, rows, start, stop):
+            o_cols = slice(o * P, (o + 1) * P)
+            columns = slice(first_padded_row * W, (first_padded_row + rows) * W)
+            nc.tensor.matmul_mx(
+                out=acc,
+                lhsT=w_codes[:, o_cols].bitcast(FP8X4),
+                lhsT_scale=w_scales[:, o_cols],
+                rhs=x_codes[:, b, columns].bitcast(FP8X4),
+                rhs_scale=x_scales[:, b, columns],
+                start=start,
+                stop=stop,
+            )
+
+        def sum_over_three_rows(b, step):
+            planes = work.tile([P, O_TILES, ROWS, ROW_PITCH], F32)
+            for o in range(O_TILES):
+                for half in range(ROWS // BANK_ROWS):
+                    top = step * ROWS + half * BANK_ROWS
+                    acc = psum.tile([P, BANK_ROWS * W], F32, tag="bank")
+                    for tap in range(3):
+                        multiply(acc[:], b, o, top + tap, BANK_ROWS, tap == 0, tap == 2)
+                    by_parity = acc[:].rearrange("p (r m e) -> p r e m", m=HALF, e=2)
+                    rows = slice(half * BANK_ROWS, (half + 1) * BANK_ROWS)
+                    nc.scalar.mul(out=planes[:, o, rows, ODD], in_=by_parity[:, :, 1, :], mul=NINTH)
+                    nc.scalar.mul(out=planes[:, o, rows, EVEN], in_=by_parity[:, :, 0, :], mul=NINTH)
+            return planes
+
+        def weigh_border_row(b, planes, at_top):
+            pair_top = 0 if at_top else H - 2
+            which = 0 if at_top else 1
+            alone = psum.tile([P, O_TILES, 2 * W], F32, tag="bank")
+            for o in range(O_TILES):
+                multiply(alone[:, o, :], b, o, pair_top + 1, 2, True, True)
+            by_parity = alone[:].rearrange("p o (r m e) -> p o r e m", r=2, e=2)
+            extra = work.tile([P, O_TILES, 1, W], F32)
+            nc.scalar.mul(out=extra[:, :, 0, 0:HALF], in_=by_parity[:, :, which, 1, :], mul=(BORDER - 1.0) * NINTH)
+            nc.scalar.mul(out=extra[:, :, 0, HALF:W], in_=by_parity[:, :, which, 0, :], mul=(BORDER - 1.0) * NINTH)
+            pair_rows = slice(pair_top % ROWS, pair_top % ROWS + 2)
+            pair = planes[:, :, pair_rows, 1 : 1 + W]
+            nc.vector.tensor_tensor(out=pair, in0=pair, in1=extra[:].to_broadcast([P, O_TILES, 2, W]), op=ADD)
+            border = planes[:, :, pair_top % ROWS + which, 1 : 1 + W]
+            nc.vector.tensor_scalar_mul(out=border, in0=border, scalar1=BORDER)
+
+        def sum_over_three_columns(planes):
+            rows = planes[:].rearrange("p o r l -> p (o r) l")
+            border = rows[:, :, HALF : HALF + 2]
+            nc.vector.tensor_scalar_mul(out=border, in0=border, scalar1=BORDER)
+            pairs = work.tile([P, O_TILES * ROWS, HALF], F32)
+            nc.vector.tensor_tensor(out=pairs[:], in0=rows[:, :, ODD], in1=rows[:, :, EVEN], op=ADD)
+            nc.vector.tensor_scalar_mul(
+                out=rows[:, :, 0 : W + 2 : W + 1], in0=pairs[:, :, 0 : HALF : HALF - 1], scalar1=BORDER - 1.0
+            )
+            third = rows.rearrange("p n (e l) -> p n l e", e=2)[:, :, 0:HALF, :]
+            result = result_pool.tile([P, O_TILES * ROWS, HALF, 2], F32)
+            nc.vector.tensor_tensor(
+                out=result[:],
+                in0=pairs[:].unsqueeze(3).to_broadcast([P, O_TILES * ROWS, HALF, 2]),
+                in1=third,
+                op=ADD,
+            )
+            return result
+
+        steps = [(b, step) for b in range(B) for step in range(STEPS_PER_IMAGE)]
+        for b, step in steps[:AHEAD]:
+            quantise_rows(b, step)
+        for n, (b, step) in enumerate(steps):
+            for later_b, later_step in steps[n + AHEAD : n + AHEAD + 1]:
+                quantise_rows(later_b, later_step)
+            planes = sum_over_three_rows(b, step)
+            if step == 0:
+                weigh_border_row(b, planes, True)
+            if step == STEPS_PER_IMAGE - 1:
+                weigh_border_row(b, planes, False)
+            result = sum_over_three_columns(planes)
+            pixels = slice(step * ROWS * W, (step + 1) * ROWS * W)
+            nc.sync.dma_start(
+                out=out[b].rearrange("(o p) h w -> p o (h w)", p=P)[:, :, pixels],
+                in_=result[:].rearrange("p (o r) m e -> p o (r m e)", o=O_TILES),
+            )

@@ -15,11 +15,11 @@ P = 128
 PACK = 4
 B, C_IN, H, W, C_OUT = 2, 512, 64, 64, 512
 O_TILES = C_OUT // P
-ROWS = 16
+ROWS = 8
 STEPS_PER_IMAGE = H // ROWS
-BANK_ROWS = 8
 HALF = W // 2
-AHEAD = 2
+RAW_BUFS = 6
+HEAD = 4
 
 BORDER = math.sqrt(1.5)
 NINTH = 1.0 / 9.0
@@ -35,24 +35,28 @@ def tile_gcn_layer_e_kernel(tc, x, weight_words, weight_scales, out):
     nc = tc.nc
     with ExitStack() as ctx:
         keep = ctx.enter_context(tc.tile_pool(name="keep", bufs=1))
-        raw_pool = ctx.enter_context(tc.tile_pool(name="raw", bufs=4))
-        grouped_pool = ctx.enter_context(tc.tile_pool(name="grouped", bufs=2))
-        work = ctx.enter_context(tc.tile_pool(name="work", bufs=2))
-        result_pool = ctx.enter_context(tc.tile_pool(name="result", bufs=3))
+        raw_pool = ctx.enter_context(tc.tile_pool(name="raw", bufs=RAW_BUFS))
+        grouped_pool = ctx.enter_context(tc.tile_pool(name="grouped", bufs=3))
+        planes_pool = ctx.enter_context(tc.tile_pool(name="planes", bufs=4))
+        work = ctx.enter_context(tc.tile_pool(name="work", bufs=3))
+        result_pool = ctx.enter_context(tc.tile_pool(name="result", bufs=4))
         psum = ctx.enter_context(tc.psum_pool(name="psum", bufs=8))
+        ctx.enter_context(tc.manual_schedule())
 
         w_codes = keep.tile([P, C_OUT], U32, align_bytes=64)
         w_scales = keep.tile([P, C_OUT], U8, align_bytes=64)
         nc.vector.memset(w_scales[:].bitcast(I32), 0)
-        nc.sync.dma_start(
-            out=w_codes[:].bitcast(I32),
-            in_=weight_words[0].rearrange("p n t -> p (n t)").bitcast(I32),
-        )
-        for quadrant in range(4):
+
+        def load_weight():
             nc.sync.dma_start(
-                out=w_scales[32 * quadrant : 32 * quadrant + 4, :].bitcast(I32),
-                in_=weight_scales[0, 4 * quadrant : 4 * quadrant + 4, :].bitcast(I32),
+                out=w_codes[:].bitcast(I32),
+                in_=weight_words[0].rearrange("p n t -> p (n t)").bitcast(I32),
             )
+            for quadrant in range(4):
+                nc.sync.dma_start(
+                    out=w_scales[32 * quadrant : 32 * quadrant + 4, :].bitcast(I32),
+                    in_=weight_scales[0, 4 * quadrant : 4 * quadrant + 4, :].bitcast(I32),
+                )
 
         x_codes = keep.tile([P, B, (H + 2) * W], U32, align_bytes=64)
         x_scales = keep.tile([P, B, (H + 2) * W], U8, align_bytes=64)
@@ -60,20 +64,31 @@ def tile_gcn_layer_e_kernel(tc, x, weight_words, weight_scales, out):
             zero_rows = padded[:].rearrange("p b (r w) -> p b r w", w=W)[:, :, 0 : H + 2 : H + 1, :]
             nc.vector.memset(zero_rows.bitcast(I32), 0)
 
-        def quantise_rows(b, step):
-            pixels = slice(step * ROWS * W, (step + 1) * ROWS * W)
+        raw_of, grouped_of, planes_of, extra_of, pairs_of = {}, {}, {}, {}, {}
+
+        def load(n):
+            b, first_row = n // STEPS_PER_IMAGE, n % STEPS_PER_IMAGE * ROWS
             raw = raw_pool.tile([P, PACK, ROWS * W], BF16)
+            pixels = slice(first_row * W, (first_row + ROWS) * W)
             nc.sync.dma_start(out=raw[:], in_=x[b].rearrange("(p t) h w -> p t (h w)", t=PACK)[:, :, pixels])
+            raw_of[n] = raw
+
+        def regroup(n):
             grouped = grouped_pool.tile([P, ROWS * W, PACK], BF16, align_bytes=64)
-            nc.scalar.copy(
+            copier = nc.vector.tensor_copy if n < HEAD and n % 2 == 1 else nc.scalar.copy
+            copier(
                 out=grouped[:].rearrange("p (c i) t -> p c t i", i=4),
-                in_=raw[:].rearrange("p t (c i) -> p c t i", i=4),
+                in_=raw_of[n][:].rearrange("p t (c i) -> p c t i", i=4),
             )
-            columns = slice((step * ROWS + 1) * W, ((step + 1) * ROWS + 1) * W)
+            grouped_of[n] = grouped
+
+        def quantise(n):
+            b, first_row = n // STEPS_PER_IMAGE, n % STEPS_PER_IMAGE * ROWS
+            columns = slice((first_row + 1) * W, (first_row + 1 + ROWS) * W)
             nc.vector.quantize_mx(
                 out=x_codes[:, b, columns].bitcast(FP8X4),
                 scales=x_scales[:, b, columns],
-                in_=grouped[:].rearrange("p n t -> p (n t)"),
+                in_=grouped_of[n][:].rearrange("p n t -> p (n t)"),
             )
 
         def multiply(acc, b, o, first_padded_row, rows, start, stop):
@@ -89,69 +104,97 @@ def tile_gcn_layer_e_kernel(tc, x, weight_words, weight_scales, out):
                 stop=stop,
             )
 
-        def sum_over_three_rows(b, step):
-            planes = work.tile([P, O_TILES, ROWS, ROW_PITCH], F32)
-            for o in range(O_TILES):
-                for half in range(ROWS // BANK_ROWS):
-                    top = step * ROWS + half * BANK_ROWS
-                    acc = psum.tile([P, BANK_ROWS * W], F32, tag="bank")
-                    for tap in range(3):
-                        multiply(acc[:], b, o, top + tap, BANK_ROWS, tap == 0, tap == 2)
-                    by_parity = acc[:].rearrange("p (r m e) -> p r e m", m=HALF, e=2)
-                    rows = slice(half * BANK_ROWS, (half + 1) * BANK_ROWS)
-                    nc.scalar.mul(out=planes[:, o, rows, ODD], in_=by_parity[:, :, 1, :], mul=NINTH)
-                    nc.scalar.mul(out=planes[:, o, rows, EVEN], in_=by_parity[:, :, 0, :], mul=NINTH)
-            return planes
+        def border_pair(n):
+            first_row = n % STEPS_PER_IMAGE * ROWS
+            if first_row == 0:
+                return 0, 0
+            if first_row == H - ROWS:
+                return ROWS - 2, 1
+            return None
 
-        def weigh_border_row(b, planes, at_top):
-            pair_top = 0 if at_top else H - 2
-            which = 0 if at_top else 1
-            alone = psum.tile([P, O_TILES, 2 * W], F32, tag="bank")
-            for o in range(O_TILES):
-                multiply(alone[:, o, :], b, o, pair_top + 1, 2, True, True)
-            by_parity = alone[:].rearrange("p o (r m e) -> p o r e m", r=2, e=2)
-            extra = work.tile([P, O_TILES, 1, W], F32)
-            nc.scalar.mul(out=extra[:, :, 0, 0:HALF], in_=by_parity[:, :, which, 1, :], mul=(BORDER - 1.0) * NINTH)
-            nc.scalar.mul(out=extra[:, :, 0, HALF:W], in_=by_parity[:, :, which, 0, :], mul=(BORDER - 1.0) * NINTH)
-            pair_rows = slice(pair_top % ROWS, pair_top % ROWS + 2)
-            pair = planes[:, :, pair_rows, 1 : 1 + W]
-            nc.vector.tensor_tensor(out=pair, in0=pair, in1=extra[:].to_broadcast([P, O_TILES, 2, W]), op=ADD)
-            border = planes[:, :, pair_top % ROWS + which, 1 : 1 + W]
-            nc.vector.tensor_scalar_mul(out=border, in0=border, scalar1=BORDER)
+        def weigh_border_columns(both):
+            nc.scalar.mul(out=both, in_=both, mul=BORDER)
 
-        def sum_over_three_columns(planes):
-            rows = planes[:].rearrange("p o r l -> p (o r) l")
-            border = rows[:, :, HALF : HALF + 2]
-            nc.vector.tensor_scalar_mul(out=border, in0=border, scalar1=BORDER)
+        def sum_over_three_rows(n):
+            b, first_row = n // STEPS_PER_IMAGE, n % STEPS_PER_IMAGE * ROWS
+            planes = planes_pool.tile([P, O_TILES, ROWS, ROW_PITCH], F32)
+            for o in range(O_TILES):
+                acc = psum.tile([P, ROWS * W], F32, tag="bank")
+                for tap in range(3):
+                    multiply(acc[:], b, o, first_row + tap, ROWS, tap == 0, tap == 2)
+                by_parity = acc[:].rearrange("p (r m e) -> p r e m", m=HALF, e=2)
+                nc.scalar.mul(out=planes[:, o, :, ODD], in_=by_parity[:, :, 1, :], mul=NINTH)
+                nc.scalar.mul(out=planes[:, o, :, EVEN], in_=by_parity[:, :, 0, :], mul=NINTH)
+            planes_of[n] = planes
+            if border_pair(n) is not None:
+                pair_top, which = border_pair(n)
+                alone = psum.tile([P, O_TILES, 2 * W], F32, tag="bank")
+                for o in range(O_TILES):
+                    multiply(alone[:, o, :], b, o, first_row + pair_top + 1, 2, True, True)
+                by_parity = alone[:].rearrange("p o (r m e) -> p o r e m", r=2, e=2)
+                extra = work.tile([P, O_TILES, 2, W], F32)
+                for row in range(2):
+                    factor = (BORDER - 1.0) * NINTH * (BORDER if row == which else 1.0)
+                    nc.scalar.mul(out=extra[:, :, row, 0:HALF], in_=by_parity[:, :, which, 1, :], mul=factor)
+                    nc.scalar.mul(out=extra[:, :, row, HALF:W], in_=by_parity[:, :, which, 0, :], mul=factor)
+                weigh_border_columns(extra[:, :, :, HALF - 1 : HALF + 1])
+                border_row = planes[:, :, pair_top + which, 1 : 1 + W]
+                nc.scalar.mul(out=border_row, in_=border_row, mul=BORDER)
+                extra_of[n] = extra
+            weigh_border_columns(planes[:, :, :, HALF : HALF + 2])
+
+
+        def add_extra(n):
+            if border_pair(n) is not None:
+                pair_top = border_pair(n)[0]
+                pair = planes_of[n][:, :, pair_top : pair_top + 2, 1 : 1 + W]
+                nc.vector.tensor_tensor(out=pair, in0=pair, in1=extra_of[n][:], op=ADD)
+
+        def add_pairs(n):
+            rows = planes_of[n][:].rearrange("p o r l -> p (o r) l")
             pairs = work.tile([P, O_TILES * ROWS, HALF], F32)
             nc.vector.tensor_tensor(out=pairs[:], in0=rows[:, :, ODD], in1=rows[:, :, EVEN], op=ADD)
+            pairs_of[n] = pairs
+
+        def fill_slots(n):
+            rows = planes_of[n][:].rearrange("p o r l -> p (o r) l")
             nc.vector.tensor_scalar_mul(
-                out=rows[:, :, 0 : W + 2 : W + 1], in0=pairs[:, :, 0 : HALF : HALF - 1], scalar1=BORDER - 1.0
+                out=rows[:, :, 0 : W + 2 : W + 1], in0=pairs_of[n][:, :, 0 : HALF : HALF - 1], scalar1=BORDER - 1.0
             )
+
+        def add_third(n):
+            b, first_row = n // STEPS_PER_IMAGE, n % STEPS_PER_IMAGE * ROWS
+            rows = planes_of[n][:].rearrange("p o r l -> p (o r) l")
             third = rows.rearrange("p n (e l) -> p n l e", e=2)[:, :, 0:HALF, :]
             result = result_pool.tile([P, O_TILES * ROWS, HALF, 2], F32)
             nc.vector.tensor_tensor(
                 out=result[:],
-                in0=pairs[:].unsqueeze(3).to_broadcast([P, O_TILES * ROWS, HALF, 2]),
+                in0=pairs_of[n][:].unsqueeze(3).to_broadcast([P, O_TILES * ROWS, HALF, 2]),
                 in1=third,
                 op=ADD,
             )
-            return result
-
-        steps = [(b, step) for b in range(B) for step in range(STEPS_PER_IMAGE)]
-        for b, step in steps[:AHEAD]:
-            quantise_rows(b, step)
-        for n, (b, step) in enumerate(steps):
-            for later_b, later_step in steps[n + AHEAD : n + AHEAD + 1]:
-                quantise_rows(later_b, later_step)
-            planes = sum_over_three_rows(b, step)
-            if step == 0:
-                weigh_border_row(b, planes, True)
-            if step == STEPS_PER_IMAGE - 1:
-                weigh_border_row(b, planes, False)
-            result = sum_over_three_columns(planes)
-            pixels = slice(step * ROWS * W, (step + 1) * ROWS * W)
-            nc.sync.dma_start(
+            pixels = slice(first_row * W, (first_row + ROWS) * W)
+            nc.gpsimd.dma_start(
                 out=out[b].rearrange("(o p) h w -> p o (h w)", p=P)[:, :, pixels],
                 in_=result[:].rearrange("p (o r) m e -> p o (r m e)", o=O_TILES),
             )
+
+        n_steps = B * STEPS_PER_IMAGE
+
+        def stage(work_of_step, n):
+            if 0 <= n < n_steps:
+                work_of_step(n)
+
+        for n in range(RAW_BUFS):
+            load(n)
+            if n == 1:
+                load_weight()
+        for turn in range(-3, n_steps + 2):
+            stage(regroup, turn + 3)
+            stage(load, turn + 3 + RAW_BUFS)
+            stage(sum_over_three_rows, turn)
+            stage(add_extra, turn - 1)
+            stage(quantise, turn + 2)
+            stage(add_pairs, turn - 1)
+            stage(add_third, turn - 2)
+            stage(fill_slots, turn - 1)

@@ -36,7 +36,7 @@ def tile_gcn_layer_e_kernel(tc, x, weight_words, weight_scales, out):
     with ExitStack() as ctx:
         keep = ctx.enter_context(tc.tile_pool(name="keep", bufs=1))
         raw_pool = ctx.enter_context(tc.tile_pool(name="raw", bufs=RAW_BUFS))
-        grouped_pool = ctx.enter_context(tc.tile_pool(name="grouped", bufs=3))
+        grouped_pool = ctx.enter_context(tc.tile_pool(name="grouped", bufs=4))
         planes_pool = ctx.enter_context(tc.tile_pool(name="planes", bufs=4))
         work = ctx.enter_context(tc.tile_pool(name="work", bufs=3))
         result_pool = ctx.enter_context(tc.tile_pool(name="result", bufs=4))
@@ -174,7 +174,7 @@ def tile_gcn_layer_e_kernel(tc, x, weight_words, weight_scales, out):
                 op=ADD,
             )
             pixels = slice(first_row * W, (first_row + ROWS) * W)
-            nc.gpsimd.dma_start(
+            nc.sync.dma_start(
                 out=out[b].rearrange("(o p) h w -> p o (h w)", p=P)[:, :, pixels],
                 in_=result[:].rearrange("p (o r) m e -> p o (r m e)", o=O_TILES),
             )
@@ -189,12 +189,12 @@ def tile_gcn_layer_e_kernel(tc, x, weight_words, weight_scales, out):
             load(n)
             if n == 1:
                 load_weight()
-        for turn in range(-3, n_steps + 2):
-            stage(regroup, turn + 3)
-            stage(load, turn + 3 + RAW_BUFS)
+        for turn in range(-4, n_steps + 2):
             stage(sum_over_three_rows, turn)
+            stage(regroup, turn + 4)
+            stage(load, turn + 4 + RAW_BUFS)
             stage(add_extra, turn - 1)
-            stage(quantise, turn + 2)
+            stage(quantise, turn + 3)
             stage(add_pairs, turn - 1)
             stage(add_third, turn - 2)
             stage(fill_slots, turn - 1)

@@ -19,7 +19,6 @@ ROWS = 8
 STEPS_PER_IMAGE = H // ROWS
 HALF = W // 2
 RAW_BUFS = 6
-HEAD = 4
 
 BORDER = math.sqrt(1.5)
 NINTH = 1.0 / 9.0
@@ -75,7 +74,7 @@ def tile_gcn_layer_e_kernel(tc, x, weight_words, weight_scales, out):
 
         def regroup(n):
             grouped = grouped_pool.tile([P, ROWS * W, PACK], BF16, align_bytes=64)
-            copier = nc.vector.tensor_copy if n < HEAD and n % 2 == 1 else nc.scalar.copy
+            copier = nc.vector.tensor_copy if n % 2 == 1 else nc.scalar.copy
             copier(
                 out=grouped[:].rearrange("p (c i) t -> p c t i", i=4),
                 in_=raw_of[n][:].rearrange("p t (c i) -> p c t i", i=4),

@@ -18,7 +18,8 @@ O_TILES = C_OUT // P
 ROWS = 8
 STEPS_PER_IMAGE = H // ROWS
 HALF = W // 2
-RAW_BUFS = 6
+RAW_BUFS = 8
+VECTOR_UNTIL = 12
 
 BORDER = math.sqrt(1.5)
 NINTH = 1.0 / 9.0
@@ -63,7 +64,12 @@ def tile_gcn_layer_e_kernel(tc, x, weight_words, weight_scales, out):
             zero_rows = padded[:].rearrange("p b (r w) -> p b r w", w=W)[:, :, 0 : H + 2 : H + 1, :]
             nc.vector.memset(zero_rows.bitcast(I32), 0)
 
+        n_steps = B * STEPS_PER_IMAGE
         raw_of, grouped_of, planes_of, extra_of, pairs_of = {}, {}, {}, {}, {}
+
+        def stage(work_of_step, n):
+            if 0 <= n < n_steps:
+                work_of_step(n)
 
         def load(n):
             b, first_row = n // STEPS_PER_IMAGE, n % STEPS_PER_IMAGE * ROWS
@@ -74,12 +80,14 @@ def tile_gcn_layer_e_kernel(tc, x, weight_words, weight_scales, out):
 
         def regroup(n):
             grouped = grouped_pool.tile([P, ROWS * W, PACK], BF16, align_bytes=64)
-            copier = nc.vector.tensor_copy if n % 2 == 1 else nc.scalar.copy
+            on_vector = n == 0 or (n % 2 == 1 and n < VECTOR_UNTIL)
+            copier = nc.vector.tensor_copy if on_vector else nc.scalar.copy
             copier(
                 out=grouped[:].rearrange("p (c i) t -> p c t i", i=4),
                 in_=raw_of[n][:].rearrange("p t (c i) -> p c t i", i=4),
             )
             grouped_of[n] = grouped
+            stage(load, n + RAW_BUFS)
 
         def quantise(n):
             b, first_row = n // STEPS_PER_IMAGE, n % STEPS_PER_IMAGE * ROWS
@@ -122,8 +130,11 @@ def tile_gcn_layer_e_kernel(tc, x, weight_words, weight_scales, out):
                 for tap in range(3):
                     multiply(acc[:], b, o, first_row + tap, ROWS, tap == 0, tap == 2)
                 by_parity = acc[:].rearrange("p (r m e) -> p r e m", m=HALF, e=2)
-                nc.scalar.mul(out=planes[:, o, :, ODD], in_=by_parity[:, :, 1, :], mul=NINTH)
-                nc.scalar.mul(out=planes[:, o, :, EVEN], in_=by_parity[:, :, 0, :], mul=NINTH)
+                nc.scalar.mul(
+                    out=planes[:, o, :, 1 : 1 + W].rearrange("p r (e m) -> p r e m", e=2),
+                    in_=by_parity[:, :, ::-1, :],
+                    mul=NINTH,
+                )
             planes_of[n] = planes
             if border_pair(n) is not None:
                 pair_top, which = border_pair(n)
@@ -178,22 +189,15 @@ def tile_gcn_layer_e_kernel(tc, x, weight_words, weight_scales, out):
                 in_=result[:].rearrange("p (o r) m e -> p o (r m e)", o=O_TILES),
             )
 
-        n_steps = B * STEPS_PER_IMAGE
-
-        def stage(work_of_step, n):
-            if 0 <= n < n_steps:
-                work_of_step(n)
-
         for n in range(RAW_BUFS):
             load(n)
             if n == 1:
                 load_weight()
-        for turn in range(-4, n_steps + 2):
+        for turn in range(-6, n_steps + 2):
             stage(sum_over_three_rows, turn)
-            stage(regroup, turn + 4)
-            stage(load, turn + 4 + RAW_BUFS)
+            stage(quantise, turn + 4)
+            stage(regroup, turn + 6)
             stage(add_extra, turn - 1)
-            stage(quantise, turn + 3)
             stage(add_pairs, turn - 1)
             stage(add_third, turn - 2)
             stage(fill_slots, turn - 1)

@@ -177,17 +177,21 @@ def tile_gcn_layer_e_kernel(tc, x, weight_words, weight_scales, out):
             rows = planes_of[n][:].rearrange("p o r l -> p (o r) l")
             third = rows.rearrange("p n (e l) -> p n l e", e=2)[:, :, 0:HALF, :]
             result = result_pool.tile([P, O_TILES * ROWS, HALF, 2], F32)
-            nc.vector.tensor_tensor(
-                out=result[:],
-                in0=pairs_of[n][:].unsqueeze(3).to_broadcast([P, O_TILES * ROWS, HALF, 2]),
-                in1=third,
-                op=ADD,
-            )
             pixels = slice(first_row * W, (first_row + ROWS) * W)
-            nc.sync.dma_start(
-                out=out[b].rearrange("(o p) h w -> p o (h w)", p=P)[:, :, pixels],
-                in_=result[:].rearrange("p (o r) m e -> p o (r m e)", o=O_TILES),
-            )
+            pieces = O_TILES if n == n_steps - 1 else 1
+            tiles = O_TILES // pieces
+            for piece in range(pieces):
+                part = slice(piece * tiles * ROWS, (piece + 1) * tiles * ROWS)
+                nc.vector.tensor_tensor(
+                    out=result[:, part],
+                    in0=pairs_of[n][:, part].unsqueeze(3).to_broadcast([P, tiles * ROWS, HALF, 2]),
+                    in1=third[:, part],
+                    op=ADD,
+                )
+                nc.sync.dma_start(
+                    out=out[b].rearrange("(o p) h w -> p o (h w)", p=P)[:, piece * tiles : (piece + 1) * tiles, pixels],
+                    in_=result[:, part].rearrange("p (o r) m e -> p o (r m e)", o=tiles),
+                )
 
         for n in range(RAW_BUFS):
             load(n)

@@ -41,7 +41,6 @@ def tile_gcn_layer_e_kernel(tc, x, weight_words, weight_scales, out):
         work = ctx.enter_context(tc.tile_pool(name="work", bufs=3))
         result_pool = ctx.enter_context(tc.tile_pool(name="result", bufs=4))
         psum = ctx.enter_context(tc.psum_pool(name="psum", bufs=8))
-        ctx.enter_context(tc.manual_schedule())
 
         w_codes = keep.tile([P, C_OUT], U32, align_bytes=64)
         w_scales = keep.tile([P, C_OUT], U8, align_bytes=64)

@@ -19,7 +19,6 @@ ROWS = 8
 STEPS_PER_IMAGE = H // ROWS
 HALF = W // 2
 RAW_BUFS = 8
-VECTOR_UNTIL = 12
 
 BORDER = math.sqrt(1.5)
 NINTH = 1.0 / 9.0
@@ -79,8 +78,7 @@ def tile_gcn_layer_e_kernel(tc, x, weight_words, weight_scales, out):
 
         def regroup(n):
             grouped = grouped_pool.tile([P, ROWS * W, PACK], BF16, align_bytes=64)
-            on_vector = n == 0 or (n % 2 == 1 and n < VECTOR_UNTIL)
-            copier = nc.vector.tensor_copy if on_vector else nc.scalar.copy
+            copier = nc.vector.tensor_copy if n < 2 else nc.any.tensor_copy
             copier(
                 out=grouped[:].rearrange("p (c i) t -> p c t i", i=4),
                 in_=raw_of[n][:].rearrange("p t (c i) -> p c t i", i=4),

from contextlib import ExitStack
import math

import concourse.mybir as mybir

BF16 = mybir.dt.bfloat16
F32 = mybir.dt.float32
I32 = mybir.dt.int32
U32 = mybir.dt.uint32
U8 = mybir.dt.uint8
FP8X4 = mybir.dt.float8_e4m3fn_x4
ADD = mybir.AluOpType.add

P = 128
PACK = 4
B, C_IN, H, W, C_OUT = 2, 512, 64, 64, 512
O_TILES = C_OUT // P
ROWS = 8
STEPS_PER_IMAGE = H // ROWS
HALF = W // 2
RAW_BUFS = 8

BORDER = math.sqrt(1.5)
NINTH = 1.0 / 9.0

ROW_PITCH = 2 * (HALF + 2)
ODD = slice(1, 1 + HALF)
EVEN = slice(1 + HALF, 1 + W)

FLOPS = 2 * B * H * W * C_IN * C_OUT


def tile_gcn_layer_e_kernel(tc, x, weight_words, weight_scales, out):
    nc = tc.nc
    with ExitStack() as ctx:
        keep = ctx.enter_context(tc.tile_pool(name="keep", bufs=1))
        raw_pool = ctx.enter_context(tc.tile_pool(name="raw", bufs=RAW_BUFS))
        grouped_pool = ctx.enter_context(tc.tile_pool(name="grouped", bufs=4))
        planes_pool = ctx.enter_context(tc.tile_pool(name="planes", bufs=4))
        work = ctx.enter_context(tc.tile_pool(name="work", bufs=3))
        result_pool = ctx.enter_context(tc.tile_pool(name="result", bufs=4))
        psum = ctx.enter_context(tc.psum_pool(name="psum", bufs=8))

        w_codes = keep.tile([P, C_OUT], U32, align_bytes=64)
        w_scales = keep.tile([P, C_OUT], U8, align_bytes=64)
        nc.vector.memset(w_scales[:].bitcast(I32), 0)

        def load_weight():
            nc.sync.dma_start(
                out=w_codes[:].bitcast(I32),
                in_=weight_words[0].rearrange("p n t -> p (n t)").bitcast(I32),
            )
            for quadrant in range(4):
                nc.sync.dma_start(
                    out=w_scales[32 * quadrant : 32 * quadrant + 4, :].bitcast(I32),
                    in_=weight_scales[0, 4 * quadrant : 4 * quadrant + 4, :].bitcast(I32),
                )

        x_codes = keep.tile([P, B, (H + 2) * W], U32, align_bytes=64)
        x_scales = keep.tile([P, B, (H + 2) * W], U8, align_bytes=64)
        for padded in (x_codes, x_scales):
            zero_rows = padded[:].rearrange("p b (r w) -> p b r w", w=W)[:, :, 0 : H + 2 : H + 1, :]
            nc.vector.memset(zero_rows.bitcast(I32), 0)

        n_steps = B * STEPS_PER_IMAGE
        raw_of, grouped_of, planes_of, extra_of, pairs_of = {}, {}, {}, {}, {}

        def stage(work_of_step, n):
            if 0 <= n < n_steps:
                work_of_step(n)

        def load(n):
            b, first_row = n // STEPS_PER_IMAGE, n % STEPS_PER_IMAGE * ROWS
            raw = raw_pool.tile([P, PACK, ROWS * W], BF16)
            pixels = slice(first_row * W, (first_row + ROWS) * W)
            nc.sync.dma_start(out=raw[:], in_=x[b].rearrange("(p t) h w -> p t (h w)", t=PACK)[:, :, pixels])
            raw_of[n] = raw

        def regroup(n):
            grouped = grouped_pool.tile([P, ROWS * W, PACK], BF16, align_bytes=64)
            copier = nc.vector.tensor_copy if n < 2 else nc.any.tensor_copy
            copier(
                out=grouped[:].rearrange("p (c i) t -> p c t i", i=4),
                in_=raw_of[n][:].rearrange("p t (c i) -> p c t i", i=4),
            )
            grouped_of[n] = grouped
            stage(load, n + RAW_BUFS)

        def quantise(n):
            b, first_row = n // STEPS_PER_IMAGE, n % STEPS_PER_IMAGE * ROWS
            columns = slice((first_row + 1) * W, (first_row + 1 + ROWS) * W)
            nc.vector.quantize_mx(
                out=x_codes[:, b, columns].bitcast(FP8X4),
                scales=x_scales[:, b, columns],
                in_=grouped_of[n][:].rearrange("p n t -> p (n t)"),
            )

        def multiply(acc, b, o, first_padded_row, rows, start, stop):
            o_cols = slice(o * P, (o + 1) * P)
            columns = slice(first_padded_row * W, (first_padded_row + rows) * W)
            nc.tensor.matmul_mx(
                out=acc,
                lhsT=w_codes[:, o_cols].bitcast(FP8X4),
                lhsT_scale=w_scales[:, o_cols],
                rhs=x_codes[:, b, columns].bitcast(FP8X4),
                rhs_scale=x_scales[:, b, columns],
                start=start,
                stop=stop,
            )

        def border_pair(n):
            first_row = n % STEPS_PER_IMAGE * ROWS
            if first_row == 0:
                return 0, 0
            if first_row == H - ROWS:
                return ROWS - 2, 1
            return None

        def weigh_border_columns(both):
            nc.scalar.mul(out=both, in_=both, mul=BORDER)

        def sum_over_three_rows(n):
            b, first_row = n // STEPS_PER_IMAGE, n % STEPS_PER_IMAGE * ROWS
            planes = planes_pool.tile([P, O_TILES, ROWS, ROW_PITCH], F32)
            for o in range(O_TILES):
                acc = psum.tile([P, ROWS * W], F32, tag="bank")
                for tap in range(3):
                    multiply(acc[:], b, o, first_row + tap, ROWS, tap == 0, tap == 2)
                by_parity = acc[:].rearrange("p (r m e) -> p r e m", m=HALF, e=2)
                nc.scalar.mul(
                    out=planes[:, o, :, 1 : 1 + W].rearrange("p r (e m) -> p r e m", e=2),
                    in_=by_parity[:, :, ::-1, :],
                    mul=NINTH,
                )
            planes_of[n] = planes
            if border_pair(n) is not None:
                pair_top, which = border_pair(n)
                alone = psum.tile([P, O_TILES, 2 * W], F32, tag="bank")
                for o in range(O_TILES):
                    multiply(alone[:, o, :], b, o, first_row + pair_top + 1, 2, True, True)
                by_parity = alone[:].rearrange("p o (r m e) -> p o r e m", r=2, e=2)
                extra = work.tile([P, O_TILES, 2, W], F32)
                for row in range(2):
                    factor = (BORDER - 1.0) * NINTH * (BORDER if row == which else 1.0)
                    nc.scalar.mul(out=extra[:, :, row, 0:HALF], in_=by_parity[:, :, which, 1, :], mul=factor)
                    nc.scalar.mul(out=extra[:, :, row, HALF:W], in_=by_parity[:, :, which, 0, :], mul=factor)
                weigh_border_columns(extra[:, :, :, HALF - 1 : HALF + 1])
                border_row = planes[:, :, pair_top + which, 1 : 1 + W]
                nc.scalar.mul(out=border_row, in_=border_row, mul=BORDER)
                extra_of[n] = extra
            weigh_border_columns(planes[:, :, :, HALF : HALF + 2])


        def add_extra(n):
            if border_pair(n) is not None:
                pair_top = border_pair(n)[0]
                pair = planes_of[n][:, :, pair_top : pair_top + 2, 1 : 1 + W]
                nc.vector.tensor_tensor(out=pair, in0=pair, in1=extra_of[n][:], op=ADD)

        def add_pairs(n):
            rows = planes_of[n][:].rearrange("p o r l -> p (o r) l")
            pairs = work.tile([P, O_TILES * ROWS, HALF], F32)
            nc.vector.tensor_tensor(out=pairs[:], in0=rows[:, :, ODD], in1=rows[:, :, EVEN], op=ADD)
            pairs_of[n] = pairs

        def fill_slots(n):
            rows = planes_of[n][:].rearrange("p o r l -> p (o r) l")
            nc.vector.tensor_scalar_mul(
                out=rows[:, :, 0 : W + 2 : W + 1], in0=pairs_of[n][:, :, 0 : HALF : HALF - 1], scalar1=BORDER - 1.0
            )

        def add_third(n):
            b, first_row = n // STEPS_PER_IMAGE, n % STEPS_PER_IMAGE * ROWS
            rows = planes_of[n][:].rearrange("p o r l -> p (o r) l")
            third = rows.rearrange("p n (e l) -> p n l e", e=2)[:, :, 0:HALF, :]
            result = result_pool.tile([P, O_TILES * ROWS, HALF, 2], F32)
            pixels = slice(first_row * W, (first_row + ROWS) * W)
            pieces = O_TILES if n == n_steps - 1 else 1
            tiles = O_TILES // pieces
            for piece in range(pieces):
                part = slice(piece * tiles * ROWS, (piece + 1) * tiles * ROWS)
                nc.vector.tensor_tensor(
                    out=result[:, part],
                    in0=pairs_of[n][:, part].unsqueeze(3).to_broadcast([P, tiles * ROWS, HALF, 2]),
                    in1=third[:, part],
                    op=ADD,
                )
                nc.sync.dma_start(
                    out=out[b].rearrange("(o p) h w -> p o (h w)", p=P)[:, piece * tiles : (piece + 1) * tiles, pixels],
                    in_=result[:, part].rearrange("p (o r) m e -> p o (r m e)", o=tiles),
                )

        for n in range(RAW_BUFS):
            load(n)
            if n == 1:
                load_weight()
        for turn in range(-6, n_steps + 2):
            stage(sum_over_three_rows, turn)
            stage(quantise, turn + 4)
            stage(regroup, turn + 6)
            stage(add_extra, turn - 1)
            stage(add_pairs, turn - 1)
            stage(add_third, turn - 2)
            stage(fill_slots, turn - 1)
